import numpy as np
import ml_dtypes


def mxq(x, axis, fmt="e4m3"):
    dtype, down = {"e4m3": (ml_dtypes.float8_e4m3fn, 7), "e5m2": (ml_dtypes.float8_e5m2, 14)}[fmt]
    v = np.moveaxis(np.asarray(x, np.float32).astype(ml_dtypes.bfloat16).astype(np.float64), axis, -1)
    blocks = v.reshape(v.shape[:-1] + (-1, 32))
    amax = np.abs(blocks).max(-1, keepdims=True)
    byte = np.maximum(np.where(amax > 0, np.frexp(amax)[1] - 1 + 127, 0) - down, 1)
    scale = np.exp2(byte - 127.0)
    codes = (blocks / scale).astype(np.float32).astype(dtype).astype(np.float64)
    return np.moveaxis((codes * scale).reshape(v.shape), -1, axis)


WIDE = False


def mx_kscale(k):
    if not WIDE:
        return np.ones(k)
    levels = np.array([10, -10, 5, -5, 0])
    a = np.random.permutation(np.resize(levels, k // 512 * 4)).reshape(k // 512, 4)
    idx = np.arange(k)
    return np.exp2(a[idx // 512, idx % 128 // 32])


BF16 = ml_dtypes.bfloat16


def bf(x):
    return np.asarray(x, np.float32).astype(BF16)


def f64(x):
    return np.asarray(x).astype(np.float64)


E2M1 = np.array([0.0, 0.5, 1.0, 1.5, 2.0, 3.0, 4.0, 6.0, -0.0, -0.5, -1.0, -1.5, -2.0, -3.0, -4.0, -6.0])


def pack_weight(w, fmt):
    k, n = w.shape
    w = f64(bf(w)).reshape(k // 32, 32, n)
    amax = np.abs(w).max(1)
    if fmt == "e4m3":
        byte = np.frexp(amax)[1] - 1 + 127 - 7
    else:
        mant, ex = np.frexp(amax / 6.0)
        byte = np.where(mant > 0.5, ex, ex - 1) + 127
    byte = np.clip(np.where(amax > 0, byte, 1), 1, 254)
    scaled = (w * np.exp2(127.0 - byte)[:, None, :]).reshape(k, n).astype(np.float32)
    by_word = np.ascontiguousarray(scaled.reshape(k // 512, 128, 4, n).transpose(0, 1, 3, 2))
    if fmt == "e4m3":
        words = by_word.astype(ml_dtypes.float8_e4m3fn).view(np.uint8)
    else:
        c = by_word.astype(ml_dtypes.float4_e2m1fn).view(np.uint8) & 0xF
        words = c[..., 0::2] | (c[..., 1::2] << 4)
    return np.ascontiguousarray(words), np.ascontiguousarray(byte.astype(np.uint8).reshape(k // 512, 16, n))


def unpack_weight(words, scales, fmt):
    g, p, n, _ = words.shape
    if fmt == "e4m3":
        vals = np.ascontiguousarray(words).view(ml_dtypes.float8_e4m3fn).astype(np.float64)
    else:
        nib = np.empty((g, p, n, 4), np.uint8)
        nib[..., 0::2] = words & 0xF
        nib[..., 1::2] = words >> 4
        vals = E2M1[nib]
    vals = vals * np.repeat(np.exp2(scales.astype(np.float64) - 127.0), 8, axis=1)[..., None]
    return vals.transpose(0, 1, 3, 2).reshape(g * 512, n)

def pack4(w):
    words, scales = pack_weight(w, "e2m1")
    return words.reshape(words.shape[0], 128, -1), scales


def unpack4(words, scales):
    return unpack_weight(words.reshape(words.shape[0], 128, -1, 2), scales, "e2m1")


B, I, H, P = 8192, 256, 256, 2048
C = I + H


def sigmoid(v):
    return 1.0 / (1.0 + np.exp(-v))


def setup_inputs():
    s = mx_kscale(C)
    x = bf(np.random.standard_normal((B, I)) * s[:I])
    rh = bf(np.random.standard_normal((B, H)) * 0.95 * s[I:])
    update = bf(np.random.standard_normal((B, H)) * 0.7)
    hidden = bf(1.5 + np.random.standard_normal((B, H)))
    Wn = np.random.standard_normal((H, C)) / np.sqrt(C) / s[None, :]
    Wn_words, Wn_scales = pack4(np.ascontiguousarray(Wn.T))
    return {"x": x,
            "rh": rh,
            "update": update,
            "hidden": hidden,
            "Wn_words": Wn_words,
            "Wn_scales": Wn_scales,
            "bn": bf(-0.1 + 0.2 * np.random.standard_normal(H)),
            "connection_strength": bf(1.0 + 0.3 * np.random.standard_normal(H)),
            "connection_decay": bf(0.4 + 0.2 * np.random.random(1)),
            "connection_history": bf(2.0 * np.random.standard_normal(H))}


def reference(x, rh, update, hidden, Wn_words, Wn_scales, bn, connection_strength, connection_decay, connection_history):
    h = f64(hidden)
    u = f64(update)
    activity = np.mean(np.abs(h), axis=0)
    ch = f64(connection_history) * f64(connection_decay) + activity
    cs = f64(connection_strength) * sigmoid(ch)
    combined_reset = np.concatenate([f64(x), f64(rh)], axis=1)
    new = (mxq(combined_reset, 1, "e4m3") @ unpack4(Wn_words, Wn_scales)) + f64(bn)
    return (1.0 - u) * h + u * new * cs[None, :]

@@ -1,0 +1,215 @@
+import concourse.mybir as mybir
+from concourse.masks import make_identity
+
+F32 = mybir.dt.float32
+BF16 = mybir.dt.bfloat16
+I32 = mybir.dt.int32
+U32 = mybir.dt.uint32
+U8 = mybir.dt.uint8
+FP8X4 = mybir.dt.float8_e4m3fn_x4
+FP4X4 = mybir.dt.float4_e2m1fn_x4
+ACT = mybir.ActivationFunctionType
+ALU = mybir.AluOpType
+
+P = 128
+ROWS = 8192
+FEAT = 256
+HALVES = FEAT // P
+BLOCKS = ROWS // P
+CHUNK = 4
+CHUNKS = BLOCKS // CHUNK
+PAIR = 2
+GROUP = 8
+GROUPS = BLOCKS // GROUP
+ONES = 32
+
+FLOPS = 2 * ROWS * 2 * FEAT * FEAT
+
+
+def tile_persistentgrucell_pb_t_kernel(
+    tc, x, rh, update, hidden, Wn_words, Wn_scales, bn,
+    connection_strength, connection_decay, connection_history, out,
+):
+    nc = tc.nc
+
+    x_v = x.rearrange("(p j) f -> p j f", j=BLOCKS)
+    rh_v = rh.rearrange("(p j) f -> p j f", j=BLOCKS)
+    u_v = update.rearrange("(p j) f -> p j f", j=BLOCKS)
+    h_v = hidden.rearrange("(p j) f -> p j f", j=BLOCKS)
+    out_v = out.rearrange("(p j) f -> p j f", j=BLOCKS)
+
+    with tc.tile_pool(name="const", bufs=1) as const, \
+            tc.tile_pool(name="keep", bufs=1) as keep, \
+            tc.tile_pool(name="h_pool", bufs=4) as h_pool, \
+            tc.tile_pool(name="abs_pool", bufs=3) as abs_pool, \
+            tc.tile_pool(name="work", bufs=2) as work, \
+            tc.tile_pool(name="mx_pool", bufs=3) as mx_pool, \
+            tc.psum_pool(name="ps_sum", bufs=1) as ps_sum, \
+            tc.psum_pool(name="ps_fwd", bufs=2) as ps_fwd, \
+            tc.psum_pool(name="ps_new", bufs=2) as ps_new, \
+            tc.psum_pool(name="ps_back", bufs=2) as ps_back:
+
+        h_tiles = []
+        u_tiles = []
+        for g in range(GROUPS):
+            blocks = slice(g * GROUP, (g + 1) * GROUP)
+            h_g = h_pool.tile([P, GROUP, FEAT], BF16, name="h_g")
+            nc.sync.dma_start(out=h_g[:], in_=h_v[:, blocks, :])
+            h_tiles.append(h_g)
+            u_g = keep.tile([P, GROUP, FEAT], BF16, name="u%d" % g)
+            nc.sync.dma_start(out=u_g[:], in_=u_v[:, blocks, :])
+            u_tiles.append(u_g)
+
+        vec_rows = const.tile([P, P], BF16, name="vec_rows")
+        nc.vector.memset(vec_rows[:], 0.0)
+        for i, vec in enumerate((bn, connection_strength, connection_history)):
+            nc.sync.dma_start(
+                out=vec_rows[HALVES * i : HALVES * (i + 1), :],
+                in_=vec.rearrange("(r c) -> r c", r=HALVES),
+            )
+        decay_bf = const.tile([P, 1], BF16, name="decay_bf")
+        nc.sync.dma_start(out=decay_bf[:], in_=connection_decay.partition_broadcast(P))
+
+        w_words = const.tile([P, 2 * FEAT], U8, name="w_words", align_bytes=64)
+        nc.sync.dma_start(out=w_words[:].bitcast(I32), in_=Wn_words[0].bitcast(I32))
+        w_scales = const.tile([P, FEAT], U8, name="w_scales", align_bytes=64)
+        nc.vector.memset(w_scales[:].bitcast(I32), 0)
+        for quadrant in range(4):
+            nc.sync.dma_start(
+                out=w_scales[32 * quadrant : 32 * quadrant + 4, :].bitcast(I32),
+                in_=Wn_scales[0, 4 * quadrant : 4 * quadrant + 4, :].bitcast(I32),
+            )
+
+        a_tiles = []
+        for c in range(CHUNKS):
+            blocks = slice(c * CHUNK, (c + 1) * CHUNK)
+            a_c = keep.tile([P, CHUNK, 2 * FEAT], BF16, name="a%d" % c)
+            nc.sync.dma_start(out=a_c[:, :, 0:FEAT], in_=x_v[:, blocks, :])
+            nc.sync.dma_start(out=a_c[:, :, FEAT : 2 * FEAT], in_=rh_v[:, blocks, :])
+            a_tiles.append(a_c)
+
+        ident_f32 = const.tile([P, P], F32, name="ident_f32")
+        make_identity(nc, ident_f32[:])
+        ident_bf = const.tile([P, P], BF16, name="ident_bf")
+        make_identity(nc, ident_bf[:])
+        ones = const.tile([P, ONES], BF16, name="ones")
+        nc.vector.memset(ones[:], 1.0)
+        warm_in = const.tile([P, 1], F32, name="warm_in")
+        nc.vector.memset(warm_in[:], 0.0)
+        warm_out = const.tile([P, 1], F32, name="warm_out")
+        nc.scalar.activation(out=warm_out[:], in_=warm_in[:], func=ACT.Sigmoid)
+
+        vec_ps = ps_back.tile([P, P], BF16, name="vec_ps", tag="back")
+        nc.tensor.transpose(vec_ps[:], vec_rows[:], ident_bf[:])
+        vec_cols = const.tile([P, 3 * HALVES], F32, name="vec_cols")
+        nc.vector.tensor_copy(out=vec_cols[:], in_=vec_ps[:, 0 : 3 * HALVES])
+        bn_cols = vec_cols[:, 0:HALVES]
+        strength_cols = vec_cols[:, HALVES : 2 * HALVES]
+        history_cols = vec_cols[:, 2 * HALVES : 3 * HALVES]
+        decay = const.tile([P, 1], F32, name="decay")
+        nc.vector.tensor_copy(out=decay[:], in_=decay_bf[:])
+        decayed = const.tile([P, HALVES], F32, name="decayed")
+        nc.vector.tensor_scalar_mul(out=decayed[:], in0=history_cols, scalar1=decay[:, 0:1])
+
+        abs_sum = [ps_sum.tile([P, ONES], F32, name="abs_sum%d" % half) for half in range(HALVES)]
+        keep_tiles = []
+        for c in range(CHUNKS):
+            g, first = divmod(c * CHUNK, GROUP)
+            h_c = h_tiles[g][:, first : first + CHUNK, :]
+            u_c = u_tiles[g][:, first : first + CHUNK, :]
+            h_abs = abs_pool.tile([P, CHUNK, FEAT], BF16, name="h_abs")
+            nc.scalar.activation(out=h_abs[:], in_=h_c, func=ACT.Abs)
+            for j in range(CHUNK):
+                for half in range(HALVES):
+                    nc.tensor.matmul(
+                        out=abs_sum[half][:],
+                        lhsT=h_abs[:, j, half * P : (half + 1) * P],
+                        rhs=ones[:],
+                        start=(c == 0 and j == 0),
+                        stop=(c == CHUNKS - 1 and j == CHUNK - 1),
+                    )
+            keep_c = keep.tile([P, CHUNK, FEAT], F32, name="keep%d" % c)
+            nc.vector.scalar_tensor_tensor(
+                out=keep_c[:], in0=u_c, scalar=1.0, in1=h_c, op0=ALU.subtract, op1=ALU.mult
+            )
+            keep_tiles.append(keep_c)
+
+        gate_in = const.tile([P, HALVES], F32, name="gate_in")
+        for half in range(HALVES):
+            nc.vector.scalar_tensor_tensor(
+                out=gate_in[:, half : half + 1],
+                in0=abs_sum[half][:, 0:1],
+                scalar=1.0 / ROWS,
+                in1=decayed[:, half : half + 1],
+                op0=ALU.mult,
+                op1=ALU.add,
+            )
+        gate = const.tile([P, HALVES], F32, name="gate")
+        nc.scalar.activation(out=gate[:], in_=gate_in[:], func=ACT.Sigmoid)
+        cs = const.tile([P, HALVES], F32, name="cs")
+        nc.vector.tensor_mul(out=cs[:], in0=gate[:], in1=strength_cols)
+        bn_cs = const.tile([P, HALVES], F32, name="bn_cs")
+        nc.vector.tensor_mul(out=bn_cs[:], in0=cs[:], in1=bn_cols)
+
+        for c in range(CHUNKS):
+            g, first = divmod(c * CHUNK, GROUP)
+            u_c = u_tiles[g][:, first : first + CHUNK, :]
+            keep_c = keep_tiles[c]
+
+            a_words = a_tiles[c][:].bitcast(F32)
+            grouped = work.tile([P, CHUNK, P, 4], BF16, name="grouped", align_bytes=64)
+            grouped_words = grouped[:].bitcast(F32)
+            for pair in range(CHUNK // PAIR):
+                fwd = ps_fwd.tile([P, PAIR, 2, P], F32, name="fwd")
+                for b in range(PAIR):
+                    for s in range(2):
+                        nc.tensor.transpose(
+                            fwd[:, b, s, :], a_words[:, pair * PAIR + b, s : FEAT : 2], ident_f32[:]
+                        )
+                nc.scalar.copy(
+                    out=grouped_words[:, pair * PAIR : (pair + 1) * PAIR, :, :],
+                    in_=fwd[:].rearrange("p b s r -> p b r s"),
+                )
+            codes = mx_pool.tile([P, CHUNK * P], U32, name="codes", align_bytes=64)
+            scales = mx_pool.tile([P, CHUNK * P], U8, name="scales", align_bytes=64)
+            nc.vector.quantize_mx(
+                out=codes[:].bitcast(FP8X4),
+                scales=scales[:],
+                in_=grouped[:].rearrange("p b r t -> p (b r t)"),
+            )
+
+            scaled = work.tile([P, HALVES, CHUNK * P], F32, name="scaled")
+            for half in range(HALVES):
+                new_ps = ps_new.tile([P, CHUNK * P], F32, name="new_ps")
+                nc.tensor.matmul_mx(
+                    out=new_ps[:],
+                    lhsT=w_words[:, half * 2 * P : (half + 1) * 2 * P].bitcast(FP4X4),
+                    lhsT_scale=w_scales[:, half * P : (half + 1) * P],
+                    rhs=codes[:].bitcast(FP8X4),
+                    rhs_scale=scales[:],
+                    start=True,
+                    stop=True,
+                )
+                nc.scalar.activation(
+                    out=scaled[:, half, :],
+                    in_=new_ps[:],
+                    func=ACT.Identity,
+                    scale=cs[:, half : half + 1],
+                    bias=bn_cs[:, half : half + 1],
+                )
+
+            gated = work.tile([P, CHUNK, FEAT], F32, name="gated")
+            for pair in range(CHUNK // PAIR):
+                back = ps_back.tile([P, PAIR, FEAT], F32, name="back")
+                for b in range(PAIR):
+                    j = pair * PAIR + b
+                    for half in range(HALVES):
+                        nc.tensor.transpose(
+                            back[:, b, half * P : (half + 1) * P],
+                            scaled[:, half, j * P : (j + 1) * P],
+                            ident_f32[:],
+                        )
+                blocks = slice(pair * PAIR, (pair + 1) * PAIR)
+                nc.vector.tensor_mul(out=gated[:, blocks, :], in0=back[:], in1=u_c[:, blocks, :])
+            nc.vector.tensor_sub(out=keep_c[:], in0=gated[:], in1=keep_c[:])
+            nc.sync.dma_start(out=out_v[:, c * CHUNK : (c + 1) * CHUNK, :], in_=keep_c[:])

@@ -1,3 +1,5 @@
+from contextlib import ExitStack
+
 import concourse.mybir as mybir
 from concourse.masks import make_identity
 
@@ -38,16 +40,26 @@ def tile_persistentgrucell_pb_t_kernel(
     h_v = hidden.rearrange("(p j) f -> p j f", j=BLOCKS)
     out_v = out.rearrange("(p j) f -> p j f", j=BLOCKS)
 
-    with tc.tile_pool(name="const", bufs=1) as const, \
-            tc.tile_pool(name="keep", bufs=1) as keep, \
-            tc.tile_pool(name="h_pool", bufs=4) as h_pool, \
-            tc.tile_pool(name="abs_pool", bufs=3) as abs_pool, \
-            tc.tile_pool(name="work", bufs=2) as work, \
-            tc.tile_pool(name="mx_pool", bufs=3) as mx_pool, \
-            tc.psum_pool(name="ps_sum", bufs=1) as ps_sum, \
-            tc.psum_pool(name="ps_fwd", bufs=2) as ps_fwd, \
-            tc.psum_pool(name="ps_new", bufs=2) as ps_new, \
-            tc.psum_pool(name="ps_back", bufs=2) as ps_back:
+    with ExitStack() as stack:
+        stack.enter_context(tc.manual_schedule())
+        const = stack.enter_context(tc.tile_pool(name="const", bufs=1))
+        keep = stack.enter_context(tc.tile_pool(name="keep", bufs=1))
+        h_pool = stack.enter_context(tc.tile_pool(name="h_pool", bufs=4))
+        abs_pool = stack.enter_context(tc.tile_pool(name="abs_pool", bufs=3))
+        work = stack.enter_context(tc.tile_pool(name="work", bufs=2))
+        mx_pool = stack.enter_context(tc.tile_pool(name="mx_pool", bufs=3))
+        ps_fwd = stack.enter_context(tc.psum_pool(name="ps_fwd", bufs=2))
+        ps_new = stack.enter_context(tc.psum_pool(name="ps_new", bufs=2))
+
+        vec_rows = const.tile([P, P], BF16, name="vec_rows")
+        nc.vector.memset(vec_rows[:], 0.0)
+        for i, vec in enumerate((bn, connection_strength, connection_history)):
+            nc.scalar.dma_start(
+                out=vec_rows[HALVES * i : HALVES * (i + 1), :],
+                in_=vec.rearrange("(r c) -> r c", r=HALVES),
+            )
+        decay_bf = const.tile([P, 1], BF16, name="decay_bf")
+        nc.scalar.dma_start(out=decay_bf[:], in_=connection_decay.partition_broadcast(P))
 
         h_tiles = []
         u_tiles = []
@@ -59,16 +71,6 @@ def tile_persistentgrucell_pb_t_kernel(
             u_g = keep.tile([P, GROUP, FEAT], BF16, name="u%d" % g)
             nc.sync.dma_start(out=u_g[:], in_=u_v[:, blocks, :])
             u_tiles.append(u_g)
-
-        vec_rows = const.tile([P, P], BF16, name="vec_rows")
-        nc.vector.memset(vec_rows[:], 0.0)
-        for i, vec in enumerate((bn, connection_strength, connection_history)):
-            nc.sync.dma_start(
-                out=vec_rows[HALVES * i : HALVES * (i + 1), :],
-                in_=vec.rearrange("(r c) -> r c", r=HALVES),
-            )
-        decay_bf = const.tile([P, 1], BF16, name="decay_bf")
-        nc.sync.dma_start(out=decay_bf[:], in_=connection_decay.partition_broadcast(P))
 
         w_words = const.tile([P, 2 * FEAT], U8, name="w_words", align_bytes=64)
         nc.sync.dma_start(out=w_words[:].bitcast(I32), in_=Wn_words[0].bitcast(I32))
@@ -88,10 +90,10 @@ def tile_persistentgrucell_pb_t_kernel(
             nc.sync.dma_start(out=a_c[:, :, FEAT : 2 * FEAT], in_=rh_v[:, blocks, :])
             a_tiles.append(a_c)
 
-        ident_f32 = const.tile([P, P], F32, name="ident_f32")
-        make_identity(nc, ident_f32[:])
         ident_bf = const.tile([P, P], BF16, name="ident_bf")
         make_identity(nc, ident_bf[:])
+        ident_f32 = const.tile([P, P], F32, name="ident_f32")
+        make_identity(nc, ident_f32[:])
         ones = const.tile([P, ONES], BF16, name="ones")
         nc.vector.memset(ones[:], 1.0)
         warm_in = const.tile([P, 1], F32, name="warm_in")
@@ -99,63 +101,73 @@ def tile_persistentgrucell_pb_t_kernel(
         warm_out = const.tile([P, 1], F32, name="warm_out")
         nc.scalar.activation(out=warm_out[:], in_=warm_in[:], func=ACT.Sigmoid)
 
-        vec_ps = ps_back.tile([P, P], BF16, name="vec_ps", tag="back")
-        nc.tensor.transpose(vec_ps[:], vec_rows[:], ident_bf[:])
-        vec_cols = const.tile([P, 3 * HALVES], F32, name="vec_cols")
-        nc.vector.tensor_copy(out=vec_cols[:], in_=vec_ps[:, 0 : 3 * HALVES])
-        bn_cols = vec_cols[:, 0:HALVES]
-        strength_cols = vec_cols[:, HALVES : 2 * HALVES]
-        history_cols = vec_cols[:, 2 * HALVES : 3 * HALVES]
-        decay = const.tile([P, 1], F32, name="decay")
-        nc.vector.tensor_copy(out=decay[:], in_=decay_bf[:])
-        decayed = const.tile([P, HALVES], F32, name="decayed")
-        nc.vector.tensor_scalar_mul(out=decayed[:], in0=history_cols, scalar1=decay[:, 0:1])
-
-        abs_sum = [ps_sum.tile([P, ONES], F32, name="abs_sum%d" % half) for half in range(HALVES)]
-        keep_tiles = []
-        for c in range(CHUNKS):
-            g, first = divmod(c * CHUNK, GROUP)
-            h_c = h_tiles[g][:, first : first + CHUNK, :]
-            u_c = u_tiles[g][:, first : first + CHUNK, :]
-            h_abs = abs_pool.tile([P, CHUNK, FEAT], BF16, name="h_abs")
-            nc.scalar.activation(out=h_abs[:], in_=h_c, func=ACT.Abs)
-            for j in range(CHUNK):
-                for half in range(HALVES):
-                    nc.tensor.matmul(
-                        out=abs_sum[half][:],
-                        lhsT=h_abs[:, j, half * P : (half + 1) * P],
-                        rhs=ones[:],
-                        start=(c == 0 and j == 0),
-                        stop=(c == CHUNKS - 1 and j == CHUNK - 1),
-                    )
-            keep_c = keep.tile([P, CHUNK, FEAT], F32, name="keep%d" % c)
-            nc.vector.scalar_tensor_tensor(
-                out=keep_c[:], in0=u_c, scalar=1.0, in1=h_c, op0=ALU.subtract, op1=ALU.mult
-            )
-            keep_tiles.append(keep_c)
-
-        gate_in = const.tile([P, HALVES], F32, name="gate_in")
-        for half in range(HALVES):
-            nc.vector.scalar_tensor_tensor(
-                out=gate_in[:, half : half + 1],
-                in0=abs_sum[half][:, 0:1],
-                scalar=1.0 / ROWS,
-                in1=decayed[:, half : half + 1],
-                op0=ALU.mult,
-                op1=ALU.add,
-            )
-        gate = const.tile([P, HALVES], F32, name="gate")
-        nc.scalar.activation(out=gate[:], in_=gate_in[:], func=ACT.Sigmoid)
         cs = const.tile([P, HALVES], F32, name="cs")
-        nc.vector.tensor_mul(out=cs[:], in0=gate[:], in1=strength_cols)
         bn_cs = const.tile([P, HALVES], F32, name="bn_cs")
-        nc.vector.tensor_mul(out=bn_cs[:], in0=cs[:], in1=bn_cols)
+        keep_tiles = []
+        with tc.psum_pool(name="ps_early", bufs=1) as ps_early:
+            vec_ps = ps_early.tile([P, P], BF16, name="vec_ps")
+            nc.tensor.transpose(vec_ps[:], vec_rows[:], ident_bf[:])
+            vec_cols = const.tile([P, 3 * HALVES], F32, name="vec_cols")
+            nc.vector.tensor_copy(out=vec_cols[:], in_=vec_ps[:, 0 : 3 * HALVES])
+            bn_cols = vec_cols[:, 0:HALVES]
+            strength_cols = vec_cols[:, HALVES : 2 * HALVES]
+            history_cols = vec_cols[:, 2 * HALVES : 3 * HALVES]
+            decay = const.tile([P, 1], F32, name="decay")
+            nc.vector.tensor_copy(out=decay[:], in_=decay_bf[:])
+            decayed = const.tile([P, HALVES], F32, name="decayed")
+            nc.vector.tensor_scalar_mul(out=decayed[:], in0=history_cols, scalar1=decay[:, 0:1])
 
-        for c in range(CHUNKS):
+            abs_sum = [
+                ps_early.tile([P, ONES], F32, name="abs_sum%d" % half) for half in range(HALVES)
+            ]
+            for c in range(CHUNKS):
+                g, first = divmod(c * CHUNK, GROUP)
+                h_c = h_tiles[g][:, first : first + CHUNK, :]
+                u_c = u_tiles[g][:, first : first + CHUNK, :]
+                h_abs = abs_pool.tile([P, CHUNK, FEAT], BF16, name="h_abs")
+                nc.scalar.activation(out=h_abs[:], in_=h_c, func=ACT.Abs)
+                for j in range(CHUNK):
+                    for half in range(HALVES):
+                        nc.tensor.matmul(
+                            out=abs_sum[half][:],
+                            lhsT=h_abs[:, j, half * P : (half + 1) * P],
+                            rhs=ones[:],
+                            start=(c == 0 and j == 0),
+                            stop=(c == CHUNKS - 1 and j == CHUNK - 1),
+                        )
+                keep_c = keep.tile([P, CHUNK, FEAT], F32, name="keep%d" % c)
+                nc.vector.scalar_tensor_tensor(
+                    out=keep_c[:], in0=u_c, scalar=1.0, in1=h_c, op0=ALU.subtract, op1=ALU.mult
+                )
+                keep_tiles.append(keep_c)
+
+            gate_in = const.tile([P, HALVES], F32, name="gate_in")
+            for half in range(HALVES):
+                nc.vector.scalar_tensor_tensor(
+                    out=gate_in[:, half : half + 1],
+                    in0=abs_sum[half][:, 0:1],
+                    scalar=1.0 / ROWS,
+                    in1=decayed[:, half : half + 1],
+                    op0=ALU.mult,
+                    op1=ALU.add,
+                )
+            gate = const.tile([P, HALVES], F32, name="gate")
+            nc.scalar.activation(out=gate[:], in_=gate_in[:], func=ACT.Sigmoid)
+            nc.vector.tensor_mul(out=cs[:], in0=gate[:], in1=strength_cols)
+            nc.vector.tensor_mul(out=bn_cs[:], in0=cs[:], in1=bn_cols)
+
+        ps_back = stack.enter_context(tc.psum_pool(name="ps_back", bufs=4))
+
+        grouped_tiles = {}
+        mx_tiles = {}
+        scaled_tiles = {}
+        gated_tiles = {}
+
+        def update_of(c):
             g, first = divmod(c * CHUNK, GROUP)
-            u_c = u_tiles[g][:, first : first + CHUNK, :]
-            keep_c = keep_tiles[c]
+            return u_tiles[g][:, first : first + CHUNK, :]
 
+        def features_to_partitions(c):
             a_words = a_tiles[c][:].bitcast(F32)
             grouped = work.tile([P, CHUNK, P, 4], BF16, name="grouped", align_bytes=64)
             grouped_words = grouped[:].bitcast(F32)
@@ -170,19 +182,27 @@ def tile_persistentgrucell_pb_t_kernel(
                     out=grouped_words[:, pair * PAIR : (pair + 1) * PAIR, :, :],
                     in_=fwd[:].rearrange("p b s r -> p b r s"),
                 )
+            grouped_tiles[c] = grouped
+
+        def quantise(c):
             codes = mx_pool.tile([P, CHUNK * P], U32, name="codes", align_bytes=64)
             scales = mx_pool.tile([P, CHUNK * P], U8, name="scales", align_bytes=64)
             nc.vector.quantize_mx(
                 out=codes[:].bitcast(FP8X4),
                 scales=scales[:],
-                in_=grouped[:].rearrange("p b r t -> p (b r t)"),
+                in_=grouped_tiles[c][:].rearrange("p b r t -> p (b r t)"),
             )
+            mx_tiles[c] = (codes, scales)
 
+        def multiply(c):
+            codes, scales = mx_tiles[c]
             scaled = work.tile([P, HALVES, CHUNK * P], F32, name="scaled")
+            new_ps = [
+                ps_new.tile([P, CHUNK * P], F32, name="new_ps") for half in range(HALVES)
+            ]
             for half in range(HALVES):
-                new_ps = ps_new.tile([P, CHUNK * P], F32, name="new_ps")
                 nc.tensor.matmul_mx(
-                    out=new_ps[:],
+                    out=new_ps[half][:],
                     lhsT=w_words[:, half * 2 * P : (half + 1) * 2 * P].bitcast(FP4X4),
                     lhsT_scale=w_scales[:, half * P : (half + 1) * P],
                     rhs=codes[:].bitcast(FP8X4),
@@ -190,14 +210,18 @@ def tile_persistentgrucell_pb_t_kernel(
                     start=True,
                     stop=True,
                 )
+            for half in range(HALVES):
                 nc.scalar.activation(
                     out=scaled[:, half, :],
-                    in_=new_ps[:],
+                    in_=new_ps[half][:],
                     func=ACT.Identity,
                     scale=cs[:, half : half + 1],
                     bias=bn_cs[:, half : half + 1],
                 )
+            scaled_tiles[c] = scaled
 
+        def rows_to_partitions_and_gate(c):
+            scaled = scaled_tiles[c]
             gated = work.tile([P, CHUNK, FEAT], F32, name="gated")
             for pair in range(CHUNK // PAIR):
                 back = ps_back.tile([P, PAIR, FEAT], F32, name="back")
@@ -210,6 +234,24 @@ def tile_persistentgrucell_pb_t_kernel(
                             ident_f32[:],
                         )
                 blocks = slice(pair * PAIR, (pair + 1) * PAIR)
-                nc.vector.tensor_mul(out=gated[:, blocks, :], in0=back[:], in1=u_c[:, blocks, :])
-            nc.vector.tensor_sub(out=keep_c[:], in0=gated[:], in1=keep_c[:])
+                nc.vector.tensor_mul(
+                    out=gated[:, blocks, :], in0=back[:], in1=update_of(c)[:, blocks, :]
+                )
+            gated_tiles[c] = gated
+
+        def blend_and_store(c):
+            keep_c = keep_tiles[c]
+            nc.vector.tensor_sub(out=keep_c[:], in0=gated_tiles[c][:], in1=keep_c[:])
             nc.sync.dma_start(out=out_v[:, c * CHUNK : (c + 1) * CHUNK, :], in_=keep_c[:])
+
+        for c in range(-2, CHUNKS):
+            if c + 2 < CHUNKS:
+                features_to_partitions(c + 2)
+            if c >= 0:
+                rows_to_partitions_and_gate(c)
+            if c + 2 < CHUNKS:
+                quantise(c + 2)
+            if 0 <= c + 1 < CHUNKS:
+                multiply(c + 1)
+            if c >= 0:
+                blend_and_store(c)

@@ -24,6 +24,9 @@ PAIR = 2
 GROUP = 8
 GROUPS = BLOCKS // GROUP
 ONES = 32
+CHUNK_COLS = CHUNK * FEAT
+POOL_COLS = 384
+VECTOR_COLS = CHUNK_COLS - POOL_COLS
 
 FLOPS = 2 * ROWS * 2 * FEAT * FEAT
 
@@ -38,7 +41,7 @@ def tile_persistentgrucell_pb_t_kernel(
     rh_v = rh.rearrange("(p j) f -> p j f", j=BLOCKS)
     u_v = update.rearrange("(p j) f -> p j f", j=BLOCKS)
     h_v = hidden.rearrange("(p j) f -> p j f", j=BLOCKS)
-    out_v = out.rearrange("(p j) f -> p j f", j=BLOCKS)
+    out_v = out.rearrange("(p j) f -> p (j f)", j=BLOCKS)
 
     with ExitStack() as stack:
         stack.enter_context(tc.manual_schedule())
@@ -222,7 +225,7 @@ def tile_persistentgrucell_pb_t_kernel(
 
         def rows_to_partitions_and_gate(c):
             scaled = scaled_tiles[c]
-            gated = work.tile([P, CHUNK, FEAT], F32, name="gated")
+            gated = a_tiles[c][:].bitcast(F32)
             for pair in range(CHUNK // PAIR):
                 back = ps_back.tile([P, PAIR, FEAT], F32, name="back")
                 for b in range(PAIR):
@@ -240,9 +243,21 @@ def tile_persistentgrucell_pb_t_kernel(
             gated_tiles[c] = gated
 
         def blend_and_store(c):
-            keep_c = keep_tiles[c]
-            nc.vector.tensor_sub(out=keep_c[:], in0=gated_tiles[c][:], in1=keep_c[:])
-            nc.sync.dma_start(out=out_v[:, c * CHUNK : (c + 1) * CHUNK, :], in_=keep_c[:])
+            kept = keep_tiles[c][:].rearrange("p b f -> p (b f)")
+            gated = gated_tiles[c].rearrange("p b f -> p (b f)")
+            nc.vector.tensor_sub(
+                out=kept[:, 0:VECTOR_COLS], in0=gated[:, 0:VECTOR_COLS], in1=kept[:, 0:VECTOR_COLS]
+            )
+            nc.gpsimd.tensor_sub(
+                out=gated[:, 0:POOL_COLS], in0=gated[:, VECTOR_COLS:], in1=kept[:, VECTOR_COLS:]
+            )
+            first = c * CHUNK_COLS
+            nc.sync.dma_start(
+                out=out_v[:, first : first + VECTOR_COLS], in_=kept[:, 0:VECTOR_COLS]
+            )
+            nc.sync.dma_start(
+                out=out_v[:, first + VECTOR_COLS : first + CHUNK_COLS], in_=gated[:, 0:POOL_COLS]
+            )
 
         for c in range(-2, CHUNKS):
             if c + 2 < CHUNKS:

@@ -50,6 +50,7 @@ def tile_persistentgrucell_pb_t_kernel(
         h_pool = stack.enter_context(tc.tile_pool(name="h_pool", bufs=4))
         abs_pool = stack.enter_context(tc.tile_pool(name="abs_pool", bufs=3))
         work = stack.enter_context(tc.tile_pool(name="work", bufs=2))
+        scaled_pool = stack.enter_context(tc.tile_pool(name="scaled_pool", bufs=3))
         mx_pool = stack.enter_context(tc.tile_pool(name="mx_pool", bufs=3))
         ps_fwd = stack.enter_context(tc.psum_pool(name="ps_fwd", bufs=2))
         ps_new = stack.enter_context(tc.psum_pool(name="ps_new", bufs=2))
@@ -199,7 +200,7 @@ def tile_persistentgrucell_pb_t_kernel(
 
         def multiply(c):
             codes, scales = mx_tiles[c]
-            scaled = work.tile([P, HALVES, CHUNK * P], F32, name="scaled")
+            scaled = scaled_pool.tile([P, HALVES, CHUNK * P], F32, name="scaled")
             new_ps = [
                 ps_new.tile([P, CHUNK * P], F32, name="new_ps") for half in range(HALVES)
             ]
@@ -259,14 +260,14 @@ def tile_persistentgrucell_pb_t_kernel(
                 out=out_v[:, first + VECTOR_COLS : first + CHUNK_COLS], in_=gated[:, 0:POOL_COLS]
             )
 
-        for c in range(-2, CHUNKS):
-            if c + 2 < CHUNKS:
-                features_to_partitions(c + 2)
+        for c in range(-3, CHUNKS):
+            if c + 3 < CHUNKS:
+                features_to_partitions(c + 3)
             if c >= 0:
                 rows_to_partitions_and_gate(c)
-            if c + 2 < CHUNKS:
-                quantise(c + 2)
-            if 0 <= c + 1 < CHUNKS:
-                multiply(c + 1)
+            if c + 3 < CHUNKS:
+                quantise(c + 3)
+            if 0 <= c + 2 < CHUNKS:
+                multiply(c + 2)
             if c >= 0:
                 blend_and_store(c)

@@ -25,7 +25,7 @@ GROUP = 8
 GROUPS = BLOCKS // GROUP
 ONES = 32
 CHUNK_COLS = CHUNK * FEAT
-POOL_COLS = 384
+POOL_COLS = 320
 VECTOR_COLS = CHUNK_COLS - POOL_COLS
 
 FLOPS = 2 * ROWS * 2 * FEAT * FEAT
@@ -246,13 +246,20 @@ def tile_persistentgrucell_pb_t_kernel(
         def blend_and_store(c):
             kept = keep_tiles[c][:].rearrange("p b f -> p (b f)")
             gated = gated_tiles[c].rearrange("p b f -> p (b f)")
+            first = c * CHUNK_COLS
+            if c == CHUNKS - 1:
+                for cols in (slice(0, CHUNK_COLS // 2), slice(CHUNK_COLS // 2, CHUNK_COLS)):
+                    nc.vector.tensor_sub(out=kept[:, cols], in0=gated[:, cols], in1=kept[:, cols])
+                    nc.sync.dma_start(
+                        out=out_v[:, first + cols.start : first + cols.stop], in_=kept[:, cols]
+                    )
+                return
             nc.vector.tensor_sub(
                 out=kept[:, 0:VECTOR_COLS], in0=gated[:, 0:VECTOR_COLS], in1=kept[:, 0:VECTOR_COLS]
             )
             nc.gpsimd.tensor_sub(
                 out=gated[:, 0:POOL_COLS], in0=gated[:, VECTOR_COLS:], in1=kept[:, VECTOR_COLS:]
             )
-            first = c * CHUNK_COLS
             nc.sync.dma_start(
                 out=out_v[:, first : first + VECTOR_COLS], in_=kept[:, 0:VECTOR_COLS]
             )

@@ -120,6 +120,8 @@ def tile_persistentgrucell_pb_t_kernel(
             nc.vector.tensor_copy(out=decay[:], in_=decay_bf[:])
             decayed = const.tile([P, HALVES], F32, name="decayed")
             nc.vector.tensor_scalar_mul(out=decayed[:], in0=history_cols, scalar1=decay[:, 0:1])
+            strength_bn = const.tile([P, HALVES], F32, name="strength_bn")
+            nc.vector.tensor_mul(out=strength_bn[:], in0=strength_cols, in1=bn_cols)
 
             abs_sum = [
                 ps_early.tile([P, ONES], F32, name="abs_sum%d" % half) for half in range(HALVES)
@@ -145,20 +147,24 @@ def tile_persistentgrucell_pb_t_kernel(
                 )
                 keep_tiles.append(keep_c)
 
-            gate_in = const.tile([P, HALVES], F32, name="gate_in")
-            for half in range(HALVES):
-                nc.vector.scalar_tensor_tensor(
-                    out=gate_in[:, half : half + 1],
-                    in0=abs_sum[half][:, 0:1],
-                    scalar=1.0 / ROWS,
-                    in1=decayed[:, half : half + 1],
-                    op0=ALU.mult,
-                    op1=ALU.add,
-                )
             gate = const.tile([P, HALVES], F32, name="gate")
-            nc.scalar.activation(out=gate[:], in_=gate_in[:], func=ACT.Sigmoid)
-            nc.vector.tensor_mul(out=cs[:], in0=gate[:], in1=strength_cols)
-            nc.vector.tensor_mul(out=bn_cs[:], in0=cs[:], in1=bn_cols)
+            for half in range(HALVES):
+                column = slice(half, half + 1)
+                nc.scalar.activation(
+                    out=gate[:, column],
+                    in_=abs_sum[half][:, 0:1],
+                    func=ACT.Sigmoid,
+                    scale=1.0 / ROWS,
+                    bias=decayed[:, column],
+                )
+                nc.scalar.activation(
+                    out=cs[:, column], in_=gate[:, column], func=ACT.Identity,
+                    scale=strength_cols[:, column],
+                )
+                nc.scalar.activation(
+                    out=bn_cs[:, column], in_=gate[:, column], func=ACT.Identity,
+                    scale=strength_bn[:, column],
+                )
 
         ps_back = stack.enter_context(tc.psum_pool(name="ps_back", bufs=4))
 

@@ -24,6 +24,8 @@ PAIR = 2
 GROUP = 8
 GROUPS = BLOCKS // GROUP
 ONES = 32
+LATE_GROUPS = 2
+EARLY_CHUNKS = (GROUPS - LATE_GROUPS) * GROUP // CHUNK
 CHUNK_COLS = CHUNK * FEAT
 POOL_COLS = 320
 VECTOR_COLS = CHUNK_COLS - POOL_COLS
@@ -67,14 +69,32 @@ def tile_persistentgrucell_pb_t_kernel(
 
         h_tiles = []
         u_tiles = []
-        for g in range(GROUPS):
-            blocks = slice(g * GROUP, (g + 1) * GROUP)
+        a_tiles = []
+
+        def load_hidden(g):
             h_g = h_pool.tile([P, GROUP, FEAT], BF16, name="h_g")
-            nc.sync.dma_start(out=h_g[:], in_=h_v[:, blocks, :])
+            nc.sync.dma_start(out=h_g[:], in_=h_v[:, g * GROUP : (g + 1) * GROUP, :])
             h_tiles.append(h_g)
+
+        def load_update(g):
             u_g = keep.tile([P, GROUP, FEAT], BF16, name="u%d" % g)
-            nc.sync.dma_start(out=u_g[:], in_=u_v[:, blocks, :])
+            nc.sync.dma_start(out=u_g[:], in_=u_v[:, g * GROUP : (g + 1) * GROUP, :])
             u_tiles.append(u_g)
+
+        def load_x_rh(c):
+            blocks = slice(c * CHUNK, (c + 1) * CHUNK)
+            a_c = keep.tile([P, CHUNK, 2 * FEAT], BF16, name="a%d" % c)
+            nc.sync.dma_start(out=a_c[:, :, 0:FEAT], in_=x_v[:, blocks, :])
+            nc.sync.dma_start(out=a_c[:, :, FEAT : 2 * FEAT], in_=rh_v[:, blocks, :])
+            a_tiles.append(a_c)
+
+        for g in range(GROUPS - LATE_GROUPS):
+            load_hidden(g)
+            load_update(g)
+        for g in range(GROUPS - LATE_GROUPS, GROUPS):
+            load_hidden(g)
+        load_x_rh(0)
+        load_x_rh(1)
 
         w_words = const.tile([P, 2 * FEAT], U8, name="w_words", align_bytes=64)
         nc.sync.dma_start(out=w_words[:].bitcast(I32), in_=Wn_words[0].bitcast(I32))
@@ -86,13 +106,10 @@ def tile_persistentgrucell_pb_t_kernel(
                 in_=Wn_scales[0, 4 * quadrant : 4 * quadrant + 4, :].bitcast(I32),
             )
 
-        a_tiles = []
-        for c in range(CHUNKS):
-            blocks = slice(c * CHUNK, (c + 1) * CHUNK)
-            a_c = keep.tile([P, CHUNK, 2 * FEAT], BF16, name="a%d" % c)
-            nc.sync.dma_start(out=a_c[:, :, 0:FEAT], in_=x_v[:, blocks, :])
-            nc.sync.dma_start(out=a_c[:, :, FEAT : 2 * FEAT], in_=rh_v[:, blocks, :])
-            a_tiles.append(a_c)
+        for c in range(2, CHUNKS):
+            if c - 2 < LATE_GROUPS:
+                load_update(GROUPS - LATE_GROUPS + c - 2)
+            load_x_rh(c)
 
         ident_bf = const.tile([P, P], BF16, name="ident_bf")
         make_identity(nc, ident_bf[:])
@@ -107,80 +124,47 @@ def tile_persistentgrucell_pb_t_kernel(
 
         cs = const.tile([P, HALVES], F32, name="cs")
         bn_cs = const.tile([P, HALVES], F32, name="bn_cs")
-        keep_tiles = []
-        with tc.psum_pool(name="ps_early", bufs=1) as ps_early:
-            vec_ps = ps_early.tile([P, P], BF16, name="vec_ps")
-            nc.tensor.transpose(vec_ps[:], vec_rows[:], ident_bf[:])
-            vec_cols = const.tile([P, 3 * HALVES], F32, name="vec_cols")
-            nc.vector.tensor_copy(out=vec_cols[:], in_=vec_ps[:, 0 : 3 * HALVES])
-            bn_cols = vec_cols[:, 0:HALVES]
-            strength_cols = vec_cols[:, HALVES : 2 * HALVES]
-            history_cols = vec_cols[:, 2 * HALVES : 3 * HALVES]
-            decay = const.tile([P, 1], F32, name="decay")
-            nc.vector.tensor_copy(out=decay[:], in_=decay_bf[:])
-            decayed = const.tile([P, HALVES], F32, name="decayed")
-            nc.vector.tensor_scalar_mul(out=decayed[:], in0=history_cols, scalar1=decay[:, 0:1])
-            strength_bn = const.tile([P, HALVES], F32, name="strength_bn")
-            nc.vector.tensor_mul(out=strength_bn[:], in0=strength_cols, in1=bn_cols)
 
-            abs_sum = [
-                ps_early.tile([P, ONES], F32, name="abs_sum%d" % half) for half in range(HALVES)
-            ]
-            for c in range(CHUNKS):
-                g, first = divmod(c * CHUNK, GROUP)
-                h_c = h_tiles[g][:, first : first + CHUNK, :]
-                u_c = u_tiles[g][:, first : first + CHUNK, :]
-                h_abs = abs_pool.tile([P, CHUNK, FEAT], BF16, name="h_abs")
-                nc.scalar.activation(out=h_abs[:], in_=h_c, func=ACT.Abs)
-                for j in range(CHUNK):
-                    for half in range(HALVES):
-                        nc.tensor.matmul(
-                            out=abs_sum[half][:],
-                            lhsT=h_abs[:, j, half * P : (half + 1) * P],
-                            rhs=ones[:],
-                            start=(c == 0 and j == 0),
-                            stop=(c == CHUNKS - 1 and j == CHUNK - 1),
-                        )
-                keep_c = keep.tile([P, CHUNK, FEAT], F32, name="keep%d" % c)
-                nc.vector.scalar_tensor_tensor(
-                    out=keep_c[:], in0=u_c, scalar=1.0, in1=h_c, op0=ALU.subtract, op1=ALU.mult
-                )
-                keep_tiles.append(keep_c)
-
-            gate = const.tile([P, HALVES], F32, name="gate")
-            for half in range(HALVES):
-                column = slice(half, half + 1)
-                nc.scalar.activation(
-                    out=gate[:, column],
-                    in_=abs_sum[half][:, 0:1],
-                    func=ACT.Sigmoid,
-                    scale=1.0 / ROWS,
-                    bias=decayed[:, column],
-                )
-                nc.scalar.activation(
-                    out=cs[:, column], in_=gate[:, column], func=ACT.Identity,
-                    scale=strength_cols[:, column],
-                )
-                nc.scalar.activation(
-                    out=bn_cs[:, column], in_=gate[:, column], func=ACT.Identity,
-                    scale=strength_bn[:, column],
-                )
-
-        ps_back = stack.enter_context(tc.psum_pool(name="ps_back", bufs=4))
-
+        keep_tiles = {}
+        fwd_tiles = {}
         grouped_tiles = {}
         mx_tiles = {}
+        new_tiles = {}
         scaled_tiles = {}
         gated_tiles = {}
+
+        def hidden_of(c):
+            g, first = divmod(c * CHUNK, GROUP)
+            return h_tiles[g][:, first : first + CHUNK, :]
 
         def update_of(c):
             g, first = divmod(c * CHUNK, GROUP)
             return u_tiles[g][:, first : first + CHUNK, :]
 
+        def add_absolute(c, abs_sum):
+            h_abs = abs_pool.tile([P, CHUNK, FEAT], BF16, name="h_abs")
+            nc.scalar.activation(out=h_abs[:], in_=hidden_of(c), func=ACT.Abs)
+            for j in range(CHUNK):
+                for half in range(HALVES):
+                    nc.tensor.matmul(
+                        out=abs_sum[half][:],
+                        lhsT=h_abs[:, j, half * P : (half + 1) * P],
+                        rhs=ones[:],
+                        start=(c == 0 and j == 0),
+                        stop=(c == CHUNKS - 1 and j == CHUNK - 1),
+                    )
+
+        def keep_part(c):
+            keep_c = keep.tile([P, CHUNK, FEAT], F32, name="keep%d" % c)
+            nc.vector.scalar_tensor_tensor(
+                out=keep_c[:], in0=update_of(c), scalar=1.0, in1=hidden_of(c),
+                op0=ALU.subtract, op1=ALU.mult,
+            )
+            keep_tiles[c] = keep_c
+
         def features_to_partitions(c):
             a_words = a_tiles[c][:].bitcast(F32)
-            grouped = work.tile([P, CHUNK, P, 4], BF16, name="grouped", align_bytes=64)
-            grouped_words = grouped[:].bitcast(F32)
+            fwd_tiles[c] = []
             for pair in range(CHUNK // PAIR):
                 fwd = ps_fwd.tile([P, PAIR, 2, P], F32, name="fwd")
                 for b in range(PAIR):
@@ -188,10 +172,18 @@ def tile_persistentgrucell_pb_t_kernel(
                         nc.tensor.transpose(
                             fwd[:, b, s, :], a_words[:, pair * PAIR + b, s : FEAT : 2], ident_f32[:]
                         )
-                nc.scalar.copy(
-                    out=grouped_words[:, pair * PAIR : (pair + 1) * PAIR, :, :],
-                    in_=fwd[:].rearrange("p b s r -> p b r s"),
-                )
+                fwd_tiles[c].append(fwd)
+
+        def group_by_four(c, on_vector=False):
+            grouped = work.tile([P, CHUNK, P, 4], BF16, name="grouped", align_bytes=64)
+            grouped_words = grouped[:].bitcast(F32)
+            for pair, fwd in enumerate(fwd_tiles[c]):
+                side_by_side = grouped_words[:, pair * PAIR : (pair + 1) * PAIR, :, :]
+                alternately = fwd[:].rearrange("p b s r -> p b r s")
+                if on_vector:
+                    nc.vector.tensor_copy(out=side_by_side, in_=alternately)
+                else:
+                    nc.scalar.copy(out=side_by_side, in_=alternately)
             grouped_tiles[c] = grouped
 
         def quantise(c):
@@ -206,7 +198,6 @@ def tile_persistentgrucell_pb_t_kernel(
 
         def multiply(c):
             codes, scales = mx_tiles[c]
-            scaled = scaled_pool.tile([P, HALVES, CHUNK * P], F32, name="scaled")
             new_ps = [
                 ps_new.tile([P, CHUNK * P], F32, name="new_ps") for half in range(HALVES)
             ]
@@ -220,10 +211,14 @@ def tile_persistentgrucell_pb_t_kernel(
                     start=True,
                     stop=True,
                 )
+            new_tiles[c] = new_ps
+
+        def scale(c):
+            scaled = scaled_pool.tile([P, HALVES, CHUNK * P], F32, name="scaled")
             for half in range(HALVES):
                 nc.scalar.activation(
                     out=scaled[:, half, :],
-                    in_=new_ps[half][:],
+                    in_=new_tiles[c][half][:],
                     func=ACT.Identity,
                     scale=cs[:, half : half + 1],
                     bias=bn_cs[:, half : half + 1],
@@ -273,14 +268,79 @@ def tile_persistentgrucell_pb_t_kernel(
                 out=out_v[:, first + VECTOR_COLS : first + CHUNK_COLS], in_=gated[:, 0:POOL_COLS]
             )
 
-        for c in range(-3, CHUNKS):
+        with tc.psum_pool(name="ps_early", bufs=1) as ps_early:
+            vec_ps = ps_early.tile([P, P], BF16, name="vec_ps")
+            nc.tensor.transpose(vec_ps[:], vec_rows[:], ident_bf[:])
+            vec_cols = const.tile([P, 3 * HALVES], F32, name="vec_cols")
+            nc.vector.tensor_copy(out=vec_cols[:], in_=vec_ps[:, 0 : 3 * HALVES])
+            bn_cols = vec_cols[:, 0:HALVES]
+            strength_cols = vec_cols[:, HALVES : 2 * HALVES]
+            history_cols = vec_cols[:, 2 * HALVES : 3 * HALVES]
+            decay = const.tile([P, 1], F32, name="decay")
+            nc.vector.tensor_copy(out=decay[:], in_=decay_bf[:])
+            decayed = const.tile([P, HALVES], F32, name="decayed")
+            nc.vector.tensor_scalar_mul(out=decayed[:], in0=history_cols, scalar1=decay[:, 0:1])
+            strength_bn = const.tile([P, HALVES], F32, name="strength_bn")
+            nc.vector.tensor_mul(out=strength_bn[:], in0=strength_cols, in1=bn_cols)
+
+            abs_sum = [
+                ps_early.tile([P, ONES], F32, name="abs_sum%d" % half) for half in range(HALVES)
+            ]
+            for c in range(EARLY_CHUNKS):
+                add_absolute(c, abs_sum)
+                keep_part(c)
+            add_absolute(EARLY_CHUNKS, abs_sum)
+            features_to_partitions(0)
+            group_by_four(0, on_vector=True)
+            add_absolute(EARLY_CHUNKS + 1, abs_sum)
+            quantise(0)
+            features_to_partitions(1)
+            for c in range(EARLY_CHUNKS + 2, CHUNKS):
+                add_absolute(c, abs_sum)
+            group_by_four(1)
+            multiply(0)
+
+            gate = const.tile([P, HALVES], F32, name="gate")
+            for half in range(HALVES):
+                column = slice(half, half + 1)
+                nc.scalar.activation(
+                    out=gate[:, column],
+                    in_=abs_sum[half][:, 0:1],
+                    func=ACT.Sigmoid,
+                    scale=1.0 / ROWS,
+                    bias=decayed[:, column],
+                )
+                nc.scalar.activation(
+                    out=cs[:, column], in_=gate[:, column], func=ACT.Identity,
+                    scale=strength_cols[:, column],
+                )
+                nc.scalar.activation(
+                    out=bn_cs[:, column], in_=gate[:, column], func=ACT.Identity,
+                    scale=strength_bn[:, column],
+                )
+
+        ps_back = stack.enter_context(tc.psum_pool(name="ps_back", bufs=4))
+
+        scale(0)
+        keep_part(EARLY_CHUNKS)
+        keep_part(EARLY_CHUNKS + 1)
+        quantise(1)
+        features_to_partitions(2)
+        group_by_four(2)
+        multiply(1)
+        scale(1)
+        for c in range(EARLY_CHUNKS + 2, CHUNKS):
+            keep_part(c)
+        quantise(2)
+
+        for c in range(CHUNKS):
             if c + 3 < CHUNKS:
                 features_to_partitions(c + 3)
-            if c >= 0:
-                rows_to_partitions_and_gate(c)
+                group_by_four(c + 3)
+            rows_to_partitions_and_gate(c)
             if c + 3 < CHUNKS:
                 quantise(c + 3)
-            if 0 <= c + 2 < CHUNKS:
+            if c + 2 < CHUNKS:
                 multiply(c + 2)
-            if c >= 0:
-                blend_and_store(c)
+                scale(c + 2)
+            blend_and_store(c)

@@ -269,6 +269,13 @@ def tile_persistentgrucell_pb_t_kernel(
             )
 
         with tc.psum_pool(name="ps_early", bufs=1) as ps_early:
+            abs_sum = [
+                ps_early.tile([P, ONES], F32, name="abs_sum%d" % half) for half in range(HALVES)
+            ]
+            for c in range(GROUP // CHUNK):
+                add_absolute(c, abs_sum)
+                keep_part(c)
+
             vec_ps = ps_early.tile([P, P], BF16, name="vec_ps")
             nc.tensor.transpose(vec_ps[:], vec_rows[:], ident_bf[:])
             vec_cols = const.tile([P, 3 * HALVES], F32, name="vec_cols")
@@ -283,10 +290,7 @@ def tile_persistentgrucell_pb_t_kernel(
             strength_bn = const.tile([P, HALVES], F32, name="strength_bn")
             nc.vector.tensor_mul(out=strength_bn[:], in0=strength_cols, in1=bn_cols)
 
-            abs_sum = [
-                ps_early.tile([P, ONES], F32, name="abs_sum%d" % half) for half in range(HALVES)
-            ]
-            for c in range(EARLY_CHUNKS):
+            for c in range(GROUP // CHUNK, EARLY_CHUNKS):
                 add_absolute(c, abs_sum)
                 keep_part(c)
             add_absolute(EARLY_CHUNKS, abs_sum)

@@ -23,7 +23,7 @@ CHUNKS = BLOCKS // CHUNK
 PAIR = 2
 GROUP = 8
 GROUPS = BLOCKS // GROUP
-ONES = 32
+ONES = 8
 LATE_GROUPS = 2
 EARLY_CHUNKS = (GROUPS - LATE_GROUPS) * GROUP // CHUNK
 CHUNK_COLS = CHUNK * FEAT
@@ -107,14 +107,16 @@ def tile_persistentgrucell_pb_t_kernel(
             )
 
         for c in range(2, CHUNKS):
-            if c - 2 < LATE_GROUPS:
-                load_update(GROUPS - LATE_GROUPS + c - 2)
+            if 0 <= c - CHUNKS // 2 < LATE_GROUPS:
+                load_update(GROUPS - LATE_GROUPS + c - CHUNKS // 2)
             load_x_rh(c)
 
         ident_bf = const.tile([P, P], BF16, name="ident_bf")
         make_identity(nc, ident_bf[:])
         ident_f32 = const.tile([P, P], F32, name="ident_f32")
         make_identity(nc, ident_f32[:])
+        minus_ident_bf = const.tile([P, P], BF16, name="minus_ident_bf")
+        nc.vector.tensor_scalar_mul(out=minus_ident_bf[:], in0=ident_bf[:], scalar1=-1.0)
         ones = const.tile([P, ONES], BF16, name="ones")
         nc.vector.memset(ones[:], 1.0)
         warm_in = const.tile([P, 1], F32, name="warm_in")
@@ -229,37 +231,65 @@ def tile_persistentgrucell_pb_t_kernel(
             scaled = scaled_tiles[c]
             gated = a_tiles[c][:].bitcast(F32)
             for pair in range(CHUNK // PAIR):
+                blocks = slice(pair * PAIR, (pair + 1) * PAIR)
                 back = ps_back.tile([P, PAIR, FEAT], F32, name="back")
+                if c >= EARLY_CHUNKS:
+                    nc.tensor.matmul(
+                        out=back[:].rearrange("p b f -> p (b f)"),
+                        lhsT=minus_ident_bf[:],
+                        rhs=hidden_of(c)[:, blocks, :].rearrange("p b f -> p (b f)"),
+                        start=True,
+                        stop=False,
+                    )
                 for b in range(PAIR):
                     j = pair * PAIR + b
                     for half in range(HALVES):
-                        nc.tensor.transpose(
-                            back[:, b, half * P : (half + 1) * P],
-                            scaled[:, half, j * P : (j + 1) * P],
-                            ident_f32[:],
-                        )
-                blocks = slice(pair * PAIR, (pair + 1) * PAIR)
+                        turned = back[:, b, half * P : (half + 1) * P]
+                        square = scaled[:, half, j * P : (j + 1) * P]
+                        if c < EARLY_CHUNKS:
+                            nc.tensor.transpose(turned, square, ident_f32[:])
+                        else:
+                            nc.tensor.matmul(
+                                out=turned,
+                                lhsT=square,
+                                rhs=ident_f32[:],
+                                is_transpose=True,
+                                start=False,
+                                stop=(b == PAIR - 1 and half == HALVES - 1),
+                            )
                 nc.vector.tensor_mul(
                     out=gated[:, blocks, :], in0=back[:], in1=update_of(c)[:, blocks, :]
                 )
             gated_tiles[c] = gated
 
         def blend_and_store(c):
-            kept = keep_tiles[c][:].rearrange("p b f -> p (b f)")
             gated = gated_tiles[c].rearrange("p b f -> p (b f)")
             first = c * CHUNK_COLS
+            if c < EARLY_CHUNKS:
+                op = ALU.subtract
+                kept = keep_tiles[c][:].rearrange("p b f -> p (b f)")
+                other = kept
+            else:
+                op = ALU.add
+                result = keep.tile([P, CHUNK, FEAT], F32, name="keep%d" % c)
+                kept = result[:].rearrange("p b f -> p (b f)")
+                other = hidden_of(c).rearrange("p b f -> p (b f)")
             if c == CHUNKS - 1:
                 for cols in (slice(0, CHUNK_COLS // 2), slice(CHUNK_COLS // 2, CHUNK_COLS)):
-                    nc.vector.tensor_sub(out=kept[:, cols], in0=gated[:, cols], in1=kept[:, cols])
+                    nc.vector.tensor_tensor(
+                        out=kept[:, cols], in0=gated[:, cols], in1=other[:, cols], op=op
+                    )
                     nc.sync.dma_start(
                         out=out_v[:, first + cols.start : first + cols.stop], in_=kept[:, cols]
                     )
                 return
-            nc.vector.tensor_sub(
-                out=kept[:, 0:VECTOR_COLS], in0=gated[:, 0:VECTOR_COLS], in1=kept[:, 0:VECTOR_COLS]
+            nc.vector.tensor_tensor(
+                out=kept[:, 0:VECTOR_COLS], in0=gated[:, 0:VECTOR_COLS], in1=other[:, 0:VECTOR_COLS],
+                op=op,
             )
-            nc.gpsimd.tensor_sub(
-                out=gated[:, 0:POOL_COLS], in0=gated[:, VECTOR_COLS:], in1=kept[:, VECTOR_COLS:]
+            nc.gpsimd.tensor_tensor(
+                out=gated[:, 0:POOL_COLS], in0=gated[:, VECTOR_COLS:], in1=other[:, VECTOR_COLS:],
+                op=op,
             )
             nc.sync.dma_start(
                 out=out_v[:, first : first + VECTOR_COLS], in_=kept[:, 0:VECTOR_COLS]
@@ -326,15 +356,11 @@ def tile_persistentgrucell_pb_t_kernel(
         ps_back = stack.enter_context(tc.psum_pool(name="ps_back", bufs=4))
 
         scale(0)
-        keep_part(EARLY_CHUNKS)
-        keep_part(EARLY_CHUNKS + 1)
         quantise(1)
         features_to_partitions(2)
         group_by_four(2)
         multiply(1)
         scale(1)
-        for c in range(EARLY_CHUNKS + 2, CHUNKS):
-            keep_part(c)
         quantise(2)
 
         for c in range(CHUNKS):

@@ -143,9 +143,18 @@ def tile_persistentgrucell_pb_t_kernel(
             g, first = divmod(c * CHUNK, GROUP)
             return u_tiles[g][:, first : first + CHUNK, :]
 
-        def add_absolute(c, abs_sum):
+        def add_absolute(c, abs_sum, on_vector=False):
             h_abs = abs_pool.tile([P, CHUNK, FEAT], BF16, name="h_abs")
-            nc.scalar.activation(out=h_abs[:], in_=hidden_of(c), func=ACT.Abs)
+            if on_vector:
+                nc.vector.tensor_scalar(
+                    out=h_abs[:].bitcast(I32),
+                    in0=hidden_of(c).bitcast(I32),
+                    scalar1=0x7FFF7FFF,
+                    scalar2=None,
+                    op0=ALU.bitwise_and,
+                )
+            else:
+                nc.scalar.activation(out=h_abs[:], in_=hidden_of(c), func=ACT.Abs)
             for j in range(CHUNK):
                 for half in range(HALVES):
                     nc.tensor.matmul(
@@ -323,15 +332,13 @@ def tile_persistentgrucell_pb_t_kernel(
             for c in range(GROUP // CHUNK, EARLY_CHUNKS):
                 add_absolute(c, abs_sum)
                 keep_part(c)
-            add_absolute(EARLY_CHUNKS, abs_sum)
+            for c in range(EARLY_CHUNKS, CHUNKS):
+                add_absolute(c, abs_sum, on_vector=True)
             features_to_partitions(0)
             group_by_four(0, on_vector=True)
-            add_absolute(EARLY_CHUNKS + 1, abs_sum)
             quantise(0)
             features_to_partitions(1)
-            for c in range(EARLY_CHUNKS + 2, CHUNKS):
-                add_absolute(c, abs_sum)
-            group_by_four(1)
+            group_by_four(1, on_vector=True)
             multiply(0)
 
             gate = const.tile([P, HALVES], F32, name="gate")
@@ -358,7 +365,7 @@ def tile_persistentgrucell_pb_t_kernel(
         scale(0)
         quantise(1)
         features_to_partitions(2)
-        group_by_four(2)
+        group_by_four(2, on_vector=True)
         multiply(1)
         scale(1)
         quantise(2)

@@ -23,9 +23,10 @@ CHUNKS = BLOCKS // CHUNK
 PAIR = 2
 GROUP = 8
 GROUPS = BLOCKS // GROUP
-ONES = 8
-LATE_GROUPS = 2
+ONES = 2
+LATE_GROUPS = 4
 EARLY_CHUNKS = (GROUPS - LATE_GROUPS) * GROUP // CHUNK
+KEPT_CHUNKS = EARLY_CHUNKS + GROUP // CHUNK
 CHUNK_COLS = CHUNK * FEAT
 POOL_COLS = 320
 VECTOR_COLS = CHUNK_COLS - POOL_COLS
@@ -49,7 +50,7 @@ def tile_persistentgrucell_pb_t_kernel(
         stack.enter_context(tc.manual_schedule())
         const = stack.enter_context(tc.tile_pool(name="const", bufs=1))
         keep = stack.enter_context(tc.tile_pool(name="keep", bufs=1))
-        h_pool = stack.enter_context(tc.tile_pool(name="h_pool", bufs=4))
+        h_pool = stack.enter_context(tc.tile_pool(name="h_pool", bufs=5))
         abs_pool = stack.enter_context(tc.tile_pool(name="abs_pool", bufs=3))
         work = stack.enter_context(tc.tile_pool(name="work", bufs=2))
         scaled_pool = stack.enter_context(tc.tile_pool(name="scaled_pool", bufs=3))
@@ -91,9 +92,10 @@ def tile_persistentgrucell_pb_t_kernel(
         for g in range(GROUPS - LATE_GROUPS):
             load_hidden(g)
             load_update(g)
-        for g in range(GROUPS - LATE_GROUPS, GROUPS):
+        for g in range(GROUPS - LATE_GROUPS, GROUPS - 1):
             load_hidden(g)
         load_x_rh(0)
+        load_hidden(GROUPS - 1)
         load_x_rh(1)
 
         w_words = const.tile([P, 2 * FEAT], U8, name="w_words", align_bytes=64)
@@ -106,9 +108,10 @@ def tile_persistentgrucell_pb_t_kernel(
                 in_=Wn_scales[0, 4 * quadrant : 4 * quadrant + 4, :].bitcast(I32),
             )
 
+        load_update(GROUPS - LATE_GROUPS)
         for c in range(2, CHUNKS):
-            if 0 <= c - CHUNKS // 2 < LATE_GROUPS:
-                load_update(GROUPS - LATE_GROUPS + c - CHUNKS // 2)
+            if 1 <= c - CHUNKS // 2 + 1 < LATE_GROUPS:
+                load_update(GROUPS - LATE_GROUPS + c - CHUNKS // 2 + 1)
             load_x_rh(c)
 
         ident_bf = const.tile([P, P], BF16, name="ident_bf")
@@ -242,7 +245,7 @@ def tile_persistentgrucell_pb_t_kernel(
             for pair in range(CHUNK // PAIR):
                 blocks = slice(pair * PAIR, (pair + 1) * PAIR)
                 back = ps_back.tile([P, PAIR, FEAT], F32, name="back")
-                if c >= EARLY_CHUNKS:
+                if c >= KEPT_CHUNKS:
                     nc.tensor.matmul(
                         out=back[:].rearrange("p b f -> p (b f)"),
                         lhsT=minus_ident_bf[:],
@@ -255,7 +258,7 @@ def tile_persistentgrucell_pb_t_kernel(
                     for half in range(HALVES):
                         turned = back[:, b, half * P : (half + 1) * P]
                         square = scaled[:, half, j * P : (j + 1) * P]
-                        if c < EARLY_CHUNKS:
+                        if c < KEPT_CHUNKS:
                             nc.tensor.transpose(turned, square, ident_f32[:])
                         else:
                             nc.tensor.matmul(
@@ -274,7 +277,7 @@ def tile_persistentgrucell_pb_t_kernel(
         def blend_and_store(c):
             gated = gated_tiles[c].rearrange("p b f -> p (b f)")
             first = c * CHUNK_COLS
-            if c < EARLY_CHUNKS:
+            if c < KEPT_CHUNKS:
                 op = ALU.subtract
                 kept = keep_tiles[c][:].rearrange("p b f -> p (b f)")
                 other = kept
@@ -332,10 +335,12 @@ def tile_persistentgrucell_pb_t_kernel(
             for c in range(GROUP // CHUNK, EARLY_CHUNKS):
                 add_absolute(c, abs_sum)
                 keep_part(c)
-            for c in range(EARLY_CHUNKS, CHUNKS):
+            for c in range(EARLY_CHUNKS, CHUNKS - GROUP // CHUNK):
                 add_absolute(c, abs_sum, on_vector=True)
             features_to_partitions(0)
-            group_by_four(0, on_vector=True)
+            group_by_four(0)
+            for c in range(CHUNKS - GROUP // CHUNK, CHUNKS):
+                add_absolute(c, abs_sum, on_vector=True)
             quantise(0)
             features_to_partitions(1)
             group_by_four(1, on_vector=True)
@@ -364,8 +369,10 @@ def tile_persistentgrucell_pb_t_kernel(
 
         scale(0)
         quantise(1)
+        for c in range(EARLY_CHUNKS, KEPT_CHUNKS):
+            keep_part(c)
         features_to_partitions(2)
-        group_by_four(2, on_vector=True)
+        group_by_four(2)
         multiply(1)
         scale(1)
         quantise(2)

@@ -65,8 +65,11 @@ def tile_persistentgrucell_pb_t_kernel(
                 out=vec_rows[HALVES * i : HALVES * (i + 1), :],
                 in_=vec.rearrange("(r c) -> r c", r=HALVES),
             )
-        decay_bf = const.tile([P, 1], BF16, name="decay_bf")
-        nc.scalar.dma_start(out=decay_bf[:], in_=connection_decay.partition_broadcast(P))
+        decay_col = const.tile([P, 1], BF16, name="decay_col")
+        nc.vector.memset(decay_col[:], 0.0)
+        nc.scalar.dma_start(
+            out=decay_col[0:1, :], in_=connection_decay.rearrange("(a b) -> a b", a=1)
+        )
 
         h_tiles = []
         u_tiles = []
@@ -92,12 +95,6 @@ def tile_persistentgrucell_pb_t_kernel(
         for g in range(GROUPS - LATE_GROUPS):
             load_hidden(g)
             load_update(g)
-        for g in range(GROUPS - LATE_GROUPS, GROUPS - 1):
-            load_hidden(g)
-        load_x_rh(0)
-        load_hidden(GROUPS - 1)
-        load_x_rh(1)
-
         w_words = const.tile([P, 2 * FEAT], U8, name="w_words", align_bytes=64)
         nc.sync.dma_start(out=w_words[:].bitcast(I32), in_=Wn_words[0].bitcast(I32))
         w_scales = const.tile([P, FEAT], U8, name="w_scales", align_bytes=64)
@@ -107,6 +104,12 @@ def tile_persistentgrucell_pb_t_kernel(
                 out=w_scales[32 * quadrant : 32 * quadrant + 4, :].bitcast(I32),
                 in_=Wn_scales[0, 4 * quadrant : 4 * quadrant + 4, :].bitcast(I32),
             )
+
+        for g in range(GROUPS - LATE_GROUPS, GROUPS - 1):
+            load_hidden(g)
+        load_x_rh(0)
+        load_hidden(GROUPS - 1)
+        load_x_rh(1)
 
         load_update(GROUPS - LATE_GROUPS)
         for c in range(2, CHUNKS):
@@ -325,10 +328,13 @@ def tile_persistentgrucell_pb_t_kernel(
             bn_cols = vec_cols[:, 0:HALVES]
             strength_cols = vec_cols[:, HALVES : 2 * HALVES]
             history_cols = vec_cols[:, 2 * HALVES : 3 * HALVES]
-            decay = const.tile([P, 1], F32, name="decay")
-            nc.vector.tensor_copy(out=decay[:], in_=decay_bf[:])
+            decay_ps = ps_early.tile([P, ONES], F32, name="decay_ps")
+            nc.tensor.matmul(
+                out=decay_ps[:], lhsT=decay_col[:, 0:1].to_broadcast([P, P]), rhs=ones[:],
+                start=True, stop=True,
+            )
             decayed = const.tile([P, HALVES], F32, name="decayed")
-            nc.vector.tensor_scalar_mul(out=decayed[:], in0=history_cols, scalar1=decay[:, 0:1])
+            nc.vector.tensor_scalar_mul(out=decayed[:], in0=history_cols, scalar1=decay_ps[:, 0:1])
             strength_bn = const.tile([P, HALVES], F32, name="strength_bn")
             nc.vector.tensor_mul(out=strength_bn[:], in0=strength_cols, in1=bn_cols)
 

@@ -28,7 +28,7 @@ LATE_GROUPS = 4
 EARLY_CHUNKS = (GROUPS - LATE_GROUPS) * GROUP // CHUNK
 KEPT_CHUNKS = EARLY_CHUNKS + GROUP // CHUNK
 CHUNK_COLS = CHUNK * FEAT
-POOL_COLS = 320
+POOL_COLS = PAIR * FEAT
 VECTOR_COLS = CHUNK_COLS - POOL_COLS
 
 FLOPS = 2 * ROWS * 2 * FEAT * FEAT
@@ -388,9 +388,9 @@ def tile_persistentgrucell_pb_t_kernel(
                 features_to_partitions(c + 3)
                 group_by_four(c + 3)
             rows_to_partitions_and_gate(c)
+            blend_and_store(c)
             if c + 3 < CHUNKS:
                 quantise(c + 3)
             if c + 2 < CHUNKS:
                 multiply(c + 2)
                 scale(c + 2)
-            blend_and_store(c)

@@ -56,7 +56,7 @@ def tile_persistentgrucell_pb_t_kernel(
         scaled_pool = stack.enter_context(tc.tile_pool(name="scaled_pool", bufs=3))
         mx_pool = stack.enter_context(tc.tile_pool(name="mx_pool", bufs=3))
         ps_fwd = stack.enter_context(tc.psum_pool(name="ps_fwd", bufs=2))
-        ps_new = stack.enter_context(tc.psum_pool(name="ps_new", bufs=2))
+        ps_new = stack.enter_context(tc.psum_pool(name="ps_new", bufs=3))
 
         vec_rows = const.tile([P, P], BF16, name="vec_rows")
         nc.vector.memset(vec_rows[:], 0.0)
@@ -148,6 +148,25 @@ def tile_persistentgrucell_pb_t_kernel(
         def update_of(c):
             g, first = divmod(c * CHUNK, GROUP)
             return u_tiles[g][:, first : first + CHUNK, :]
+
+        def add_group_absolute(g, abs_sum):
+            h_abs = abs_pool.tile([P, GROUP, FEAT], BF16, name="h_abs_group")
+            nc.vector.tensor_scalar(
+                out=h_abs[:].bitcast(I32),
+                in0=h_tiles[g][:].bitcast(I32),
+                scalar1=0x7FFF7FFF,
+                scalar2=None,
+                op0=ALU.bitwise_and,
+            )
+            for j in range(GROUP):
+                for half in range(HALVES):
+                    nc.tensor.matmul(
+                        out=abs_sum[half][:],
+                        lhsT=h_abs[:, j, half * P : (half + 1) * P],
+                        rhs=ones[:],
+                        start=False,
+                        stop=(g == GROUPS - 1 and j == GROUP - 1),
+                    )
 
         def add_absolute(c, abs_sum, on_vector=False):
             h_abs = abs_pool.tile([P, CHUNK, FEAT], BF16, name="h_abs")
@@ -290,7 +309,10 @@ def tile_persistentgrucell_pb_t_kernel(
                 kept = result[:].rearrange("p b f -> p (b f)")
                 other = hidden_of(c).rearrange("p b f -> p (b f)")
             if c == CHUNKS - 1:
-                for cols in (slice(0, CHUNK_COLS // 2), slice(CHUNK_COLS // 2, CHUNK_COLS)):
+                half, quarter = CHUNK_COLS // 2, CHUNK_COLS // 4
+                for cols in (
+                    slice(0, half), slice(half, half + quarter), slice(half + quarter, CHUNK_COLS)
+                ):
                     nc.vector.tensor_tensor(
                         out=kept[:, cols], in0=gated[:, cols], in1=other[:, cols], op=op
                     )
@@ -321,14 +343,14 @@ def tile_persistentgrucell_pb_t_kernel(
                 add_absolute(c, abs_sum)
                 keep_part(c)
 
-            vec_ps = ps_early.tile([P, P], BF16, name="vec_ps")
+            vec_ps = ps_new.tile([P, P], BF16, name="new_ps")
             nc.tensor.transpose(vec_ps[:], vec_rows[:], ident_bf[:])
             vec_cols = const.tile([P, 3 * HALVES], F32, name="vec_cols")
             nc.vector.tensor_copy(out=vec_cols[:], in_=vec_ps[:, 0 : 3 * HALVES])
             bn_cols = vec_cols[:, 0:HALVES]
             strength_cols = vec_cols[:, HALVES : 2 * HALVES]
             history_cols = vec_cols[:, 2 * HALVES : 3 * HALVES]
-            decay_ps = ps_early.tile([P, ONES], F32, name="decay_ps")
+            decay_ps = ps_new.tile([P, ONES], F32, name="new_ps")
             nc.tensor.matmul(
                 out=decay_ps[:], lhsT=decay_col[:, 0:1].to_broadcast([P, P]), rhs=ones[:],
                 start=True, stop=True,
@@ -341,8 +363,8 @@ def tile_persistentgrucell_pb_t_kernel(
             for c in range(GROUP // CHUNK, EARLY_CHUNKS):
                 add_absolute(c, abs_sum)
                 keep_part(c)
-            for c in range(EARLY_CHUNKS, CHUNKS - GROUP // CHUNK):
-                add_absolute(c, abs_sum, on_vector=True)
+            for g in range(GROUPS - LATE_GROUPS, GROUPS - 1):
+                add_group_absolute(g, abs_sum)
             features_to_partitions(0)
             group_by_four(0)
             for c in range(CHUNKS - GROUP // CHUNK, CHUNKS):
@@ -371,7 +393,7 @@ def tile_persistentgrucell_pb_t_kernel(
                     scale=strength_bn[:, column],
                 )
 
-        ps_back = stack.enter_context(tc.psum_pool(name="ps_back", bufs=4))
+        ps_back = stack.enter_context(tc.psum_pool(name="ps_back", bufs=3))
 
         scale(0)
         quantise(1)

from contextlib import ExitStack

import concourse.mybir as mybir
from concourse.masks import make_identity

F32 = mybir.dt.float32
BF16 = mybir.dt.bfloat16
I32 = mybir.dt.int32
U32 = mybir.dt.uint32
U8 = mybir.dt.uint8
FP8X4 = mybir.dt.float8_e4m3fn_x4
FP4X4 = mybir.dt.float4_e2m1fn_x4
ACT = mybir.ActivationFunctionType
ALU = mybir.AluOpType

P = 128
ROWS = 8192
FEAT = 256
HALVES = FEAT // P
BLOCKS = ROWS // P
CHUNK = 4
CHUNKS = BLOCKS // CHUNK
PAIR = 2
GROUP = 8
GROUPS = BLOCKS // GROUP
ONES = 2
LATE_GROUPS = 4
EARLY_CHUNKS = (GROUPS - LATE_GROUPS) * GROUP // CHUNK
KEPT_CHUNKS = EARLY_CHUNKS + GROUP // CHUNK
CHUNK_COLS = CHUNK * FEAT
POOL_COLS = PAIR * FEAT
VECTOR_COLS = CHUNK_COLS - POOL_COLS

FLOPS = 2 * ROWS * 2 * FEAT * FEAT


def tile_persistentgrucell_pb_t_kernel(
    tc, x, rh, update, hidden, Wn_words, Wn_scales, bn,
    connection_strength, connection_decay, connection_history, out,
):
    nc = tc.nc

    x_v = x.rearrange("(p j) f -> p j f", j=BLOCKS)
    rh_v = rh.rearrange("(p j) f -> p j f", j=BLOCKS)
    u_v = update.rearrange("(p j) f -> p j f", j=BLOCKS)
    h_v = hidden.rearrange("(p j) f -> p j f", j=BLOCKS)
    out_v = out.rearrange("(p j) f -> p (j f)", j=BLOCKS)

    with ExitStack() as stack:
        stack.enter_context(tc.manual_schedule())
        const = stack.enter_context(tc.tile_pool(name="const", bufs=1))
        keep = stack.enter_context(tc.tile_pool(name="keep", bufs=1))
        h_pool = stack.enter_context(tc.tile_pool(name="h_pool", bufs=5))
        abs_pool = stack.enter_context(tc.tile_pool(name="abs_pool", bufs=3))
        work = stack.enter_context(tc.tile_pool(name="work", bufs=2))
        scaled_pool = stack.enter_context(tc.tile_pool(name="scaled_pool", bufs=3))
        mx_pool = stack.enter_context(tc.tile_pool(name="mx_pool", bufs=3))
        ps_fwd = stack.enter_context(tc.psum_pool(name="ps_fwd", bufs=2))
        ps_new = stack.enter_context(tc.psum_pool(name="ps_new", bufs=3))

        vec_rows = const.tile([P, P], BF16, name="vec_rows")
        nc.vector.memset(vec_rows[:], 0.0)
        for i, vec in enumerate((bn, connection_strength, connection_history)):
            nc.scalar.dma_start(
                out=vec_rows[HALVES * i : HALVES * (i + 1), :],
                in_=vec.rearrange("(r c) -> r c", r=HALVES),
            )
        decay_col = const.tile([P, 1], BF16, name="decay_col")
        nc.vector.memset(decay_col[:], 0.0)
        nc.scalar.dma_start(
            out=decay_col[0:1, :], in_=connection_decay.rearrange("(a b) -> a b", a=1)
        )

        h_tiles = []
        u_tiles = []
        a_tiles = []

        def load_hidden(g):
            h_g = h_pool.tile([P, GROUP, FEAT], BF16, name="h_g")
            nc.sync.dma_start(out=h_g[:], in_=h_v[:, g * GROUP : (g + 1) * GROUP, :])
            h_tiles.append(h_g)

        def load_update(g):
            u_g = keep.tile([P, GROUP, FEAT], BF16, name="u%d" % g)
            nc.sync.dma_start(out=u_g[:], in_=u_v[:, g * GROUP : (g + 1) * GROUP, :])
            u_tiles.append(u_g)

        def load_x_rh(c):
            blocks = slice(c * CHUNK, (c + 1) * CHUNK)
            a_c = keep.tile([P, CHUNK, 2 * FEAT], BF16, name="a%d" % c)
            nc.sync.dma_start(out=a_c[:, :, 0:FEAT], in_=x_v[:, blocks, :])
            nc.sync.dma_start(out=a_c[:, :, FEAT : 2 * FEAT], in_=rh_v[:, blocks, :])
            a_tiles.append(a_c)

        for g in range(GROUPS - LATE_GROUPS):
            load_hidden(g)
            load_update(g)
        w_words = const.tile([P, 2 * FEAT], U8, name="w_words", align_bytes=64)
        nc.sync.dma_start(out=w_words[:].bitcast(I32), in_=Wn_words[0].bitcast(I32))
        w_scales = const.tile([P, FEAT], U8, name="w_scales", align_bytes=64)
        nc.vector.memset(w_scales[:].bitcast(I32), 0)
        for quadrant in range(4):
            nc.sync.dma_start(
                out=w_scales[32 * quadrant : 32 * quadrant + 4, :].bitcast(I32),
                in_=Wn_scales[0, 4 * quadrant : 4 * quadrant + 4, :].bitcast(I32),
            )

        for g in range(GROUPS - LATE_GROUPS, GROUPS - 1):
            load_hidden(g)
        load_x_rh(0)
        load_hidden(GROUPS - 1)
        load_x_rh(1)

        load_update(GROUPS - LATE_GROUPS)
        for c in range(2, CHUNKS):
            if 1 <= c - CHUNKS // 2 + 1 < LATE_GROUPS:
                load_update(GROUPS - LATE_GROUPS + c - CHUNKS // 2 + 1)
            load_x_rh(c)

        ident_bf = const.tile([P, P], BF16, name="ident_bf")
        make_identity(nc, ident_bf[:])
        ident_f32 = const.tile([P, P], F32, name="ident_f32")
        make_identity(nc, ident_f32[:])
        minus_ident_bf = const.tile([P, P], BF16, name="minus_ident_bf")
        nc.vector.tensor_scalar_mul(out=minus_ident_bf[:], in0=ident_bf[:], scalar1=-1.0)
        ones = const.tile([P, ONES], BF16, name="ones")
        nc.vector.memset(ones[:], 1.0)
        warm_in = const.tile([P, 1], F32, name="warm_in")
        nc.vector.memset(warm_in[:], 0.0)
        warm_out = const.tile([P, 1], F32, name="warm_out")
        nc.scalar.activation(out=warm_out[:], in_=warm_in[:], func=ACT.Sigmoid)

        cs = const.tile([P, HALVES], F32, name="cs")
        bn_cs = const.tile([P, HALVES], F32, name="bn_cs")

        keep_tiles = {}
        fwd_tiles = {}
        grouped_tiles = {}
        mx_tiles = {}
        new_tiles = {}
        scaled_tiles = {}
        gated_tiles = {}

        def hidden_of(c):
            g, first = divmod(c * CHUNK, GROUP)
            return h_tiles[g][:, first : first + CHUNK, :]

        def update_of(c):
            g, first = divmod(c * CHUNK, GROUP)
            return u_tiles[g][:, first : first + CHUNK, :]

        def add_group_absolute(g, abs_sum):
            h_abs = abs_pool.tile([P, GROUP, FEAT], BF16, name="h_abs_group")
            nc.vector.tensor_scalar(
                out=h_abs[:].bitcast(I32),
                in0=h_tiles[g][:].bitcast(I32),
                scalar1=0x7FFF7FFF,
                scalar2=None,
                op0=ALU.bitwise_and,
            )
            for j in range(GROUP):
                for half in range(HALVES):
                    nc.tensor.matmul(
                        out=abs_sum[half][:],
                        lhsT=h_abs[:, j, half * P : (half + 1) * P],
                        rhs=ones[:],
                        start=False,
                        stop=(g == GROUPS - 1 and j == GROUP - 1),
                    )

        def add_absolute(c, abs_sum, on_vector=False):
            h_abs = abs_pool.tile([P, CHUNK, FEAT], BF16, name="h_abs")
            if on_vector:
                nc.vector.tensor_scalar(
                    out=h_abs[:].bitcast(I32),
                    in0=hidden_of(c).bitcast(I32),
                    scalar1=0x7FFF7FFF,
                    scalar2=None,
                    op0=ALU.bitwise_and,
                )
            else:
                nc.scalar.activation(out=h_abs[:], in_=hidden_of(c), func=ACT.Abs)
            for j in range(CHUNK):
                for half in range(HALVES):
                    nc.tensor.matmul(
                        out=abs_sum[half][:],
                        lhsT=h_abs[:, j, half * P : (half + 1) * P],
                        rhs=ones[:],
                        start=(c == 0 and j == 0),
                        stop=(c == CHUNKS - 1 and j == CHUNK - 1),
                    )

        def keep_part(c):
            keep_c = keep.tile([P, CHUNK, FEAT], F32, name="keep%d" % c)
            nc.vector.scalar_tensor_tensor(
                out=keep_c[:], in0=update_of(c), scalar=1.0, in1=hidden_of(c),
                op0=ALU.subtract, op1=ALU.mult,
            )
            keep_tiles[c] = keep_c

        def features_to_partitions(c):
            a_words = a_tiles[c][:].bitcast(F32)
            fwd_tiles[c] = []
            for pair in range(CHUNK // PAIR):
                fwd = ps_fwd.tile([P, PAIR, 2, P], F32, name="fwd")
                for b in range(PAIR):
                    for s in range(2):
                        nc.tensor.transpose(
                            fwd[:, b, s, :], a_words[:, pair * PAIR + b, s : FEAT : 2], ident_f32[:]
                        )
                fwd_tiles[c].append(fwd)

        def group_by_four(c, on_vector=False):
            grouped = work.tile([P, CHUNK, P, 4], BF16, name="grouped", align_bytes=64)
            grouped_words = grouped[:].bitcast(F32)
            for pair, fwd in enumerate(fwd_tiles[c]):
                side_by_side = grouped_words[:, pair * PAIR : (pair + 1) * PAIR, :, :]
                alternately = fwd[:].rearrange("p b s r -> p b r s")
                if on_vector:
                    nc.vector.tensor_copy(out=side_by_side, in_=alternately)
                else:
                    nc.scalar.copy(out=side_by_side, in_=alternately)
            grouped_tiles[c] = grouped

        def quantise(c):
            codes = mx_pool.tile([P, CHUNK * P], U32, name="codes", align_bytes=64)
            scales = mx_pool.tile([P, CHUNK * P], U8, name="scales", align_bytes=64)
            nc.vector.quantize_mx(
                out=codes[:].bitcast(FP8X4),
                scales=scales[:],
                in_=grouped_tiles[c][:].rearrange("p b r t -> p (b r t)"),
            )
            mx_tiles[c] = (codes, scales)

        def multiply(c):
            codes, scales = mx_tiles[c]
            new_ps = [
                ps_new.tile([P, CHUNK * P], F32, name="new_ps") for half in range(HALVES)
            ]
            for half in range(HALVES):
                nc.tensor.matmul_mx(
                    out=new_ps[half][:],
                    lhsT=w_words[:, half * 2 * P : (half + 1) * 2 * P].bitcast(FP4X4),
                    lhsT_scale=w_scales[:, half * P : (half + 1) * P],
                    rhs=codes[:].bitcast(FP8X4),
                    rhs_scale=scales[:],
                    start=True,
                    stop=True,
                )
            new_tiles[c] = new_ps

        def scale(c):
            scaled = scaled_pool.tile([P, HALVES, CHUNK * P], F32, name="scaled")
            for half in range(HALVES):
                nc.scalar.activation(
                    out=scaled[:, half, :],
                    in_=new_tiles[c][half][:],
                    func=ACT.Identity,
                    scale=cs[:, half : half + 1],
                    bias=bn_cs[:, half : half + 1],
                )
            scaled_tiles[c] = scaled

        def rows_to_partitions_and_gate(c):
            scaled = scaled_tiles[c]
            gated = a_tiles[c][:].bitcast(F32)
            for pair in range(CHUNK // PAIR):
                blocks = slice(pair * PAIR, (pair + 1) * PAIR)
                back = ps_back.tile([P, PAIR, FEAT], F32, name="back")
                if c >= KEPT_CHUNKS:
                    nc.tensor.matmul(
                        out=back[:].rearrange("p b f -> p (b f)"),
                        lhsT=minus_ident_bf[:],
                        rhs=hidden_of(c)[:, blocks, :].rearrange("p b f -> p (b f)"),
                        start=True,
                        stop=False,
                    )
                for b in range(PAIR):
                    j = pair * PAIR + b
                    for half in range(HALVES):
                        turned = back[:, b, half * P : (half + 1) * P]
                        square = scaled[:, half, j * P : (j + 1) * P]
                        if c < KEPT_CHUNKS:
                            nc.tensor.transpose(turned, square, ident_f32[:])
                        else:
                            nc.tensor.matmul(
                                out=turned,
                                lhsT=square,
                                rhs=ident_f32[:],
                                is_transpose=True,
                                start=False,
                                stop=(b == PAIR - 1 and half == HALVES - 1),
                            )
                nc.vector.tensor_mul(
                    out=gated[:, blocks, :], in0=back[:], in1=update_of(c)[:, blocks, :]
                )
            gated_tiles[c] = gated

        def blend_and_store(c):
            gated = gated_tiles[c].rearrange("p b f -> p (b f)")
            first = c * CHUNK_COLS
            if c < KEPT_CHUNKS:
                op = ALU.subtract
                kept = keep_tiles[c][:].rearrange("p b f -> p (b f)")
                other = kept
            else:
                op = ALU.add
                result = keep.tile([P, CHUNK, FEAT], F32, name="keep%d" % c)
                kept = result[:].rearrange("p b f -> p (b f)")
                other = hidden_of(c).rearrange("p b f -> p (b f)")
            if c == CHUNKS - 1:
                half, quarter = CHUNK_COLS // 2, CHUNK_COLS // 4
                for cols in (
                    slice(0, half), slice(half, half + quarter), slice(half + quarter, CHUNK_COLS)
                ):
                    nc.vector.tensor_tensor(
                        out=kept[:, cols], in0=gated[:, cols], in1=other[:, cols], op=op
                    )
                    nc.sync.dma_start(
                        out=out_v[:, first + cols.start : first + cols.stop], in_=kept[:, cols]
                    )
                return
            nc.vector.tensor_tensor(
                out=kept[:, 0:VECTOR_COLS], in0=gated[:, 0:VECTOR_COLS], in1=other[:, 0:VECTOR_COLS],
                op=op,
            )
            nc.gpsimd.tensor_tensor(
                out=gated[:, 0:POOL_COLS], in0=gated[:, VECTOR_COLS:], in1=other[:, VECTOR_COLS:],
                op=op,
            )
            nc.sync.dma_start(
                out=out_v[:, first : first + VECTOR_COLS], in_=kept[:, 0:VECTOR_COLS]
            )
            nc.sync.dma_start(
                out=out_v[:, first + VECTOR_COLS : first + CHUNK_COLS], in_=gated[:, 0:POOL_COLS]
            )

        with tc.psum_pool(name="ps_early", bufs=1) as ps_early:
            abs_sum = [
                ps_early.tile([P, ONES], F32, name="abs_sum%d" % half) for half in range(HALVES)
            ]
            for c in range(GROUP // CHUNK):
                add_absolute(c, abs_sum)
                keep_part(c)

            vec_ps = ps_new.tile([P, P], BF16, name="new_ps")
            nc.tensor.transpose(vec_ps[:], vec_rows[:], ident_bf[:])
            vec_cols = const.tile([P, 3 * HALVES], F32, name="vec_cols")
            nc.vector.tensor_copy(out=vec_cols[:], in_=vec_ps[:, 0 : 3 * HALVES])
            bn_cols = vec_cols[:, 0:HALVES]
            strength_cols = vec_cols[:, HALVES : 2 * HALVES]
            history_cols = vec_cols[:, 2 * HALVES : 3 * HALVES]
            decay_ps = ps_new.tile([P, ONES], F32, name="new_ps")
            nc.tensor.matmul(
                out=decay_ps[:], lhsT=decay_col[:, 0:1].to_broadcast([P, P]), rhs=ones[:],
                start=True, stop=True,
            )
            decayed = const.tile([P, HALVES], F32, name="decayed")
            nc.vector.tensor_scalar_mul(out=decayed[:], in0=history_cols, scalar1=decay_ps[:, 0:1])
            strength_bn = const.tile([P, HALVES], F32, name="strength_bn")
            nc.vector.tensor_mul(out=strength_bn[:], in0=strength_cols, in1=bn_cols)

            for c in range(GROUP // CHUNK, EARLY_CHUNKS):
                add_absolute(c, abs_sum)
                keep_part(c)
            for g in range(GROUPS - LATE_GROUPS, GROUPS - 1):
                add_group_absolute(g, abs_sum)
            features_to_partitions(0)
            group_by_four(0)
            for c in range(CHUNKS - GROUP // CHUNK, CHUNKS):
                add_absolute(c, abs_sum, on_vector=True)
            quantise(0)
            features_to_partitions(1)
            group_by_four(1, on_vector=True)
            multiply(0)

            gate = const.tile([P, HALVES], F32, name="gate")
            for half in range(HALVES):
                column = slice(half, half + 1)
                nc.scalar.activation(
                    out=gate[:, column],
                    in_=abs_sum[half][:, 0:1],
                    func=ACT.Sigmoid,
                    scale=1.0 / ROWS,
                    bias=decayed[:, column],
                )
                nc.scalar.activation(
                    out=cs[:, column], in_=gate[:, column], func=ACT.Identity,
                    scale=strength_cols[:, column],
                )
                nc.scalar.activation(
                    out=bn_cs[:, column], in_=gate[:, column], func=ACT.Identity,
                    scale=strength_bn[:, column],
                )

        ps_back = stack.enter_context(tc.psum_pool(name="ps_back", bufs=3))

        scale(0)
        quantise(1)
        for c in range(EARLY_CHUNKS, KEPT_CHUNKS):
            keep_part(c)
        features_to_partitions(2)
        group_by_four(2)
        multiply(1)
        scale(1)
        quantise(2)

        for c in range(CHUNKS):
            if c + 3 < CHUNKS:
                features_to_partitions(c + 3)
                group_by_four(c + 3)
            rows_to_partitions_and_gate(c)
            blend_and_store(c)
            if c + 3 < CHUNKS:
                quantise(c + 3)
            if c + 2 < CHUNKS:
                multiply(c + 2)
                scale(c + 2)
